import numpy as np
import ml_dtypes


def mxq(x, axis, fmt="e4m3"):
    dtype, down = {"e4m3": (ml_dtypes.float8_e4m3fn, 7), "e5m2": (ml_dtypes.float8_e5m2, 14)}[fmt]
    v = np.moveaxis(np.asarray(x, np.float32).astype(ml_dtypes.bfloat16).astype(np.float64), axis, -1)
    blocks = v.reshape(v.shape[:-1] + (-1, 32))
    amax = np.abs(blocks).max(-1, keepdims=True)
    byte = np.maximum(np.where(amax > 0, np.frexp(amax)[1] - 1 + 127, 0) - down, 1)
    scale = np.exp2(byte - 127.0)
    codes = (blocks / scale).astype(np.float32).astype(dtype).astype(np.float64)
    return np.moveaxis((codes * scale).reshape(v.shape), -1, axis)


WIDE = False


def mx_kscale(k):
    if not WIDE:
        return np.ones(k)
    levels = np.array([10, -10, 5, -5, 0])
    a = np.random.permutation(np.resize(levels, k // 512 * 4)).reshape(k // 512, 4)
    idx = np.arange(k)
    return np.exp2(a[idx // 512, idx % 128 // 32])


BF16 = ml_dtypes.bfloat16


def bf(x):
    return np.asarray(x, np.float32).astype(BF16)


def f64(x):
    return np.asarray(x).astype(np.float64)


B, S, DIM, HEADS = 1, 512, 2048, 16
HD = DIM // HEADS
EPS = 1e-6


def rms_norm(x, g):
    var = np.mean(np.square(x), axis=-1, keepdims=True)
    return x * (1.0 / np.sqrt(var + EPS)) * g


def rope(x, cos, sin):
    x1, x2 = np.split(x, 2, axis=-1)
    rot = np.concatenate([-x2, x1], axis=-1)
    return x * cos[None, :, None, :] + rot * sin[None, :, None, :]


def setup_inputs():
    s = mx_kscale(DIM)
    return {
        "hidden_states": bf(np.random.standard_normal((B, S, DIM)) * s),
        "cos": bf(np.random.uniform(-1.0, 1.0, (S, HD))),
        "sin": bf(np.random.uniform(-1.0, 1.0, (S, HD))),
        "w_qk": bf(np.random.standard_normal((DIM + DIM, DIM)) / np.sqrt(DIM) / s[None, :]),
        "b_qk": bf(np.random.standard_normal(DIM + DIM) * 0.2),
        "g_q": bf(1.0 + 0.1 * np.random.standard_normal(DIM)),
        "g_k": bf(1.0 + 0.1 * np.random.standard_normal(DIM)),
    }


def reference(hidden_states, cos, sin, w_qk, b_qk, g_q, g_k):
    c, sn = f64(cos), f64(sin)
    qk = (mxq(f64(hidden_states), 2, "e4m3") @ mxq(f64(w_qk), 1, "e4m3").T) + f64(b_qk)
    q = rms_norm(qk[:, :, :DIM], f64(g_q)).reshape(B, S, HEADS, HD)
    k = rms_norm(qk[:, :, DIM:], f64(g_k)).reshape(B, S, HEADS, HD)
    return rope(q, c, sn), rope(k, c, sn)

@@ -1,0 +1,282 @@
+from contextlib import ExitStack
+
+import concourse.mybir as mybir
+from concourse.masks import make_identity
+
+F32 = mybir.dt.float32
+BF16 = mybir.dt.bfloat16
+U32 = mybir.dt.uint32
+U8 = mybir.dt.uint8
+FP8X4 = mybir.dt.float8_e4m3fn_x4
+ACT = mybir.ActivationFunctionType
+ALU = mybir.AluOpType
+AXIS = mybir.AxisListType
+
+P = 128
+TOKENS = 512
+TOKEN_TILES = TOKENS // P
+DIM = 2048
+HEAD_DIM = 128
+HALF_DIM = HEAD_DIM // 2
+HEADS = DIM // HEAD_DIM
+ALL_HEADS = 2 * HEADS
+K_PASS = 4 * P
+PASSES = DIM // K_PASS
+WORDS = K_PASS // 2
+HEADS_PER_LOAD = 4
+EPS = 1e-6
+
+FLOPS = 2 * TOKENS * 2 * DIM * DIM
+
+
+def tile_dynamicselfattention_pa_kernel(
+    tc, hidden_states, cos, sin, w_qk, b_qk, g_q, g_k, out_0, out_1
+):
+    nc = tc.nc
+    hidden_rows = hidden_states.flatten_outer_dims()
+    outs = [
+        out_0.rearrange("b s h d -> (b s) (h d)"),
+        out_1.rearrange("b s h d -> (b s) (h d)"),
+    ]
+
+    with ExitStack() as ctx:
+        const = ctx.enter_context(tc.tile_pool(name="const", bufs=1))
+        hidden_pool = ctx.enter_context(tc.tile_pool(name="hidden", bufs=TOKEN_TILES))
+        weight_pool = ctx.enter_context(tc.tile_pool(name="weight", bufs=3))
+        stage = ctx.enter_context(tc.tile_pool(name="stage", bufs=3))
+        result_pool = ctx.enter_context(tc.tile_pool(name="result", bufs=2))
+        flipped_pool = ctx.enter_context(tc.psum_pool(name="flipped", bufs=4))
+        acc_pool = ctx.enter_context(tc.psum_pool(name="acc", bufs=2))
+        back_pool = ctx.enter_context(tc.psum_pool(name="back", bufs=2))
+
+        ident = const.tile([P, P], F32)
+        make_identity(nc, ident[:])
+
+        eps_col = const.tile([P, 1], F32)
+        nc.vector.memset(eps_col[:], EPS)
+        warm = const.tile([P, 1], F32)
+        nc.scalar.activation(out=warm[:], in_=eps_col[:], func=ACT.Sqrt)
+
+        hidden_tiles = []
+        for t in range(TOKEN_TILES):
+            h_rows = hidden_pool.tile([P, DIM], BF16, name="h_rows")
+            nc.sync.dma_start(out=h_rows[:], in_=hidden_rows[t * P : (t + 1) * P, :])
+            hidden_tiles.append(h_rows)
+
+        vec_rows_bf = const.tile([P, P], BF16)
+        nc.vector.memset(vec_rows_bf[:], 0.0)
+        nc.scalar.dma_start(
+            out=vec_rows_bf[0:ALL_HEADS, :], in_=b_qk.rearrange("(h d) -> h d", d=HEAD_DIM)
+        )
+        nc.scalar.dma_start(
+            out=vec_rows_bf[ALL_HEADS : ALL_HEADS + HEADS, :],
+            in_=g_q.rearrange("(h d) -> h d", d=HEAD_DIM),
+        )
+        nc.scalar.dma_start(
+            out=vec_rows_bf[ALL_HEADS + HEADS : 2 * ALL_HEADS, :],
+            in_=g_k.rearrange("(h d) -> h d", d=HEAD_DIM),
+        )
+        cos_bf = const.tile([P, TOKEN_TILES, HEAD_DIM], BF16)
+        nc.scalar.dma_start(out=cos_bf[:], in_=cos.rearrange("(t p) d -> p t d", p=P))
+        sin_bf = const.tile([P, TOKEN_TILES, HEAD_DIM], BF16)
+        nc.scalar.dma_start(out=sin_bf[:], in_=sin.rearrange("(t p) d -> p t d", p=P))
+
+        vec_rows = const.tile([P, P], F32)
+        nc.vector.tensor_copy(out=vec_rows[:], in_=vec_rows_bf[:])
+        vec_cols_ps = back_pool.tile([P, TOKEN_TILES, HEAD_DIM], F32, tag="back")
+        nc.tensor.transpose(vec_cols_ps[:, 0, :], vec_rows[:], ident[:])
+        vec_cols = const.tile([P, P], F32)
+        nc.vector.tensor_copy(out=vec_cols[:], in_=vec_cols_ps[:, 0, :])
+        bias_col = vec_cols[:, 0:ALL_HEADS]
+        gain_col = vec_cols[:, ALL_HEADS : 2 * ALL_HEADS]
+        gain_bias_col = const.tile([P, ALL_HEADS], F32)
+        nc.vector.tensor_tensor(out=gain_bias_col[:], in0=bias_col, in1=gain_col, op=ALU.mult)
+
+        cos_f = const.tile([P, TOKEN_TILES, HEAD_DIM], F32)
+        nc.vector.tensor_copy(out=cos_f[:], in_=cos_bf[:])
+        sin_signed = const.tile([P, TOKEN_TILES, HEAD_DIM], F32)
+        nc.vector.tensor_scalar(
+            out=sin_signed[:, :, 0:HALF_DIM],
+            in0=sin_bf[:, :, 0:HALF_DIM],
+            scalar1=-1.0,
+            scalar2=None,
+            op0=ALU.mult,
+        )
+        nc.vector.tensor_copy(
+            out=sin_signed[:, :, HALF_DIM:HEAD_DIM], in_=sin_bf[:, :, HALF_DIM:HEAD_DIM]
+        )
+
+        def words_to_partitions(rows_words, grouped_words):
+            for pair in range(PASSES // 2):
+                flipped = flipped_pool.tile([P, 2, 2, P], F32, name="flipped")
+                for g2 in range(2):
+                    for u in range(2):
+                        first = (2 * pair + g2) * WORDS + u * P
+                        nc.tensor.transpose(
+                            flipped[:, g2, u, :], rows_words[:, first : first + P], ident[:]
+                        )
+                nc.scalar.copy(
+                    out=grouped_words[:, 2 * pair : 2 * pair + 2, :, :],
+                    in_=flipped[:].rearrange("p g u r -> p g r u"),
+                )
+
+        h_grouped = const.tile([P, PASSES * TOKENS * 4], BF16, align_bytes=64)
+        h_grouped_words = (
+            h_grouped[:].bitcast(F32).rearrange("p (g s u) -> p g s u", g=PASSES, u=2)
+        )
+        h_codes = const.tile([P, PASSES * TOKENS], U32, align_bytes=64)
+        h_scales = const.tile([P, PASSES * TOKENS], U8, align_bytes=64)
+        for t in range(TOKEN_TILES):
+            words_to_partitions(
+                hidden_tiles[t][:].bitcast(F32), h_grouped_words[:, :, t * P : (t + 1) * P, :]
+            )
+        for g in range(PASSES):
+            nc.vector.quantize_mx(
+                out=h_codes[:, g * TOKENS : (g + 1) * TOKENS].bitcast(FP8X4),
+                scales=h_scales[:, g * TOKENS : (g + 1) * TOKENS],
+                in_=h_grouped[:, g * TOKENS * 4 : (g + 1) * TOKENS * 4],
+            )
+
+        weight_rows = {}
+        grouped_of = {}
+        codes_of = {}
+        acc_of = {}
+        scaled_of = {}
+        square_sum = {}
+        rotated = {}
+
+        def flip(head):
+            load, j = divmod(head, HEADS_PER_LOAD)
+            if j == 0:
+                w_rows = weight_pool.tile([P, HEADS_PER_LOAD, DIM], BF16, name="w_rows")
+                first = load * HEADS_PER_LOAD * P
+                nc.sync.dma_start(
+                    out=w_rows[:],
+                    in_=w_qk[first : first + HEADS_PER_LOAD * P, :].rearrange(
+                        "(j c) k -> c j k", c=P
+                    ),
+                )
+                weight_rows[load] = w_rows
+            w_grouped = stage.tile([P, PASSES * P * 4], BF16, name="w_grouped", align_bytes=64)
+            words_to_partitions(
+                weight_rows[load][:, j, :].bitcast(F32),
+                w_grouped[:].bitcast(F32).rearrange("p (g c u) -> p g c u", g=PASSES, u=2),
+            )
+            grouped_of[head] = w_grouped
+
+        def quantise(head):
+            w_codes = stage.tile([P, PASSES * P], U32, name="w_codes", align_bytes=64)
+            w_scales = stage.tile([P, PASSES * P], U8, name="w_scales", align_bytes=64)
+            nc.vector.quantize_mx(
+                out=w_codes[:].bitcast(FP8X4), scales=w_scales[:], in_=grouped_of[head][:]
+            )
+            codes_of[head] = (w_codes, w_scales)
+
+        def multiply(head):
+            w_codes, w_scales = codes_of[head]
+            acc = acc_pool.tile([P, TOKENS], F32, name="acc")
+            for g in range(PASSES):
+                nc.tensor.matmul_mx(
+                    out=acc[:],
+                    lhsT=w_codes[:, g * P : (g + 1) * P].bitcast(FP8X4),
+                    lhsT_scale=w_scales[:, g * P : (g + 1) * P],
+                    rhs=h_codes[:, g * TOKENS : (g + 1) * TOKENS].bitcast(FP8X4),
+                    rhs_scale=h_scales[:, g * TOKENS : (g + 1) * TOKENS],
+                    start=(g == 0),
+                    stop=(g == PASSES - 1),
+                )
+            acc_of[head] = acc
+
+        def bias_gain_square(head):
+            half, h = divmod(head, HEADS)
+            acc = acc_of[head]
+            scaled = stage.tile([P, TOKENS], F32, name="scaled")
+            nc.scalar.activation(
+                out=scaled[:],
+                in_=acc[:],
+                func=ACT.Identity,
+                bias=gain_bias_col[:, head : head + 1],
+                scale=gain_col[:, head : head + 1],
+            )
+            scaled_of[head] = scaled
+            if h == 0:
+                square = result_pool.tile([P, TOKENS], F32, name="square_sum")
+                square_sum[half] = square
+            else:
+                square = stage.tile([P, TOKENS], F32, name="square")
+            nc.scalar.activation(
+                out=square[:],
+                in_=acc[:],
+                func=ACT.Square,
+                bias=bias_col[:, head : head + 1],
+                scale=1.0,
+            )
+            if h > 0:
+                nc.gpsimd.tensor_tensor(
+                    out=square_sum[half][:], in0=square_sum[half][:], in1=square[:], op=ALU.add
+                )
+
+        def rotate(head):
+            half, h = divmod(head, HEADS)
+            if h == 0:
+                rotated[half] = result_pool.tile(
+                    [P, TOKEN_TILES, HEADS, HEAD_DIM], F32, name="rotated"
+                )
+            back = back_pool.tile([P, TOKEN_TILES, HEAD_DIM], F32, name="back")
+            for t in range(TOKEN_TILES):
+                nc.tensor.transpose(
+                    back[:, t, :], scaled_of[head][:, t * P : (t + 1) * P], ident[:]
+                )
+            straight = stage.tile([P, TOKEN_TILES, HEAD_DIM], F32, name="straight")
+            nc.vector.tensor_tensor(out=straight[:], in0=back[:], in1=cos_f[:], op=ALU.mult)
+            crossed = stage.tile([P, TOKEN_TILES, HEAD_DIM], F32, name="crossed")
+            nc.vector.tensor_tensor(
+                out=crossed[:, :, 0:HALF_DIM],
+                in0=back[:, :, HALF_DIM:HEAD_DIM],
+                in1=sin_signed[:, :, 0:HALF_DIM],
+                op=ALU.mult,
+            )
+            nc.vector.tensor_tensor(
+                out=crossed[:, :, HALF_DIM:HEAD_DIM],
+                in0=back[:, :, 0:HALF_DIM],
+                in1=sin_signed[:, :, HALF_DIM:HEAD_DIM],
+                op=ALU.mult,
+            )
+            nc.vector.tensor_tensor(
+                out=rotated[half][:, :, h, :], in0=straight[:], in1=crossed[:], op=ALU.add
+            )
+
+        def normalise_and_store(half):
+            sums_back = back_pool.tile([P, TOKEN_TILES, HEAD_DIM], F32, name="back")
+            for t in range(TOKEN_TILES):
+                nc.tensor.transpose(
+                    sums_back[:, t, :], square_sum[half][:, t * P : (t + 1) * P], ident[:]
+                )
+            total = stage.tile([P, TOKEN_TILES], F32, name="total")
+            nc.vector.tensor_reduce(out=total[:], in_=sums_back[:], axis=AXIS.X, op=ALU.add)
+            rms = stage.tile([P, TOKEN_TILES], F32, name="rms")
+            nc.scalar.activation(
+                out=rms[:], in_=total[:], func=ACT.Sqrt, bias=eps_col[:, 0:1], scale=1.0 / DIM
+            )
+            inv_rms = stage.tile([P, TOKEN_TILES], F32, name="inv_rms")
+            nc.vector.reciprocal(out=inv_rms[:], in_=rms[:])
+            for t in range(TOKEN_TILES):
+                row = rotated[half][:, t, :, :].rearrange("p h d -> p (h d)")
+                nc.vector.tensor_scalar(
+                    out=row, in0=row, scalar1=inv_rms[:, t : t + 1], scalar2=None, op0=ALU.mult
+                )
+                nc.sync.dma_start(out=outs[half][t * P : (t + 1) * P, :], in_=row)
+
+        for step in range(ALL_HEADS + 3):
+            if 0 <= step - 1 < ALL_HEADS:
+                quantise(step - 1)
+            if 0 <= step - 3:
+                rotate(step - 3)
+                if (step - 3) % HEADS == HEADS - 1:
+                    normalise_and_store((step - 3) // HEADS)
+            if 0 <= step - 2 < ALL_HEADS:
+                bias_gain_square(step - 2)
+            if step < ALL_HEADS:
+                flip(step)
+            if 0 <= step - 1 < ALL_HEADS:
+                multiply(step - 1)

@@ -23,7 +23,7 @@ ALL_HEADS = 2 * HEADS
 K_PASS = 4 * P
 PASSES = DIM // K_PASS
 WORDS = K_PASS // 2
-HEADS_PER_LOAD = 4
+PREFETCH = 6
 EPS = 1e-6
 
 FLOPS = 2 * TOKENS * 2 * DIM * DIM
@@ -42,26 +42,28 @@ def tile_dynamicselfattention_pa_kernel(
     with ExitStack() as ctx:
         const = ctx.enter_context(tc.tile_pool(name="const", bufs=1))
         hidden_pool = ctx.enter_context(tc.tile_pool(name="hidden", bufs=TOKEN_TILES))
-        weight_pool = ctx.enter_context(tc.tile_pool(name="weight", bufs=3))
+        weight_pool = ctx.enter_context(tc.tile_pool(name="weight", bufs=PREFETCH + 2))
         stage = ctx.enter_context(tc.tile_pool(name="stage", bufs=3))
         result_pool = ctx.enter_context(tc.tile_pool(name="result", bufs=2))
         flipped_pool = ctx.enter_context(tc.psum_pool(name="flipped", bufs=4))
         acc_pool = ctx.enter_context(tc.psum_pool(name="acc", bufs=2))
         back_pool = ctx.enter_context(tc.psum_pool(name="back", bufs=2))
+        ctx.enter_context(tc.manual_schedule())
 
-        ident = const.tile([P, P], F32)
-        make_identity(nc, ident[:])
+        weight_rows = {}
+        grouped_of = {}
+        codes_of = {}
+        acc_of = {}
+        scaled_of = {}
+        square_sum = {}
+        rotated = {}
+        inv_rms_of = {}
+        total_of = {}
 
-        eps_col = const.tile([P, 1], F32)
-        nc.vector.memset(eps_col[:], EPS)
-        warm = const.tile([P, 1], F32)
-        nc.scalar.activation(out=warm[:], in_=eps_col[:], func=ACT.Sqrt)
-
-        hidden_tiles = []
-        for t in range(TOKEN_TILES):
-            h_rows = hidden_pool.tile([P, DIM], BF16, name="h_rows")
-            nc.sync.dma_start(out=h_rows[:], in_=hidden_rows[t * P : (t + 1) * P, :])
-            hidden_tiles.append(h_rows)
+        def load_weights(head):
+            w_rows = weight_pool.tile([P, DIM], BF16, name="w_rows")
+            nc.sync.dma_start(out=w_rows[:], in_=w_qk[head * P : (head + 1) * P, :])
+            weight_rows[head] = w_rows
 
         vec_rows_bf = const.tile([P, P], BF16)
         nc.vector.memset(vec_rows_bf[:], 0.0)
@@ -80,6 +82,54 @@ def tile_dynamicselfattention_pa_kernel(
         nc.scalar.dma_start(out=cos_bf[:], in_=cos.rearrange("(t p) d -> p t d", p=P))
         sin_bf = const.tile([P, TOKEN_TILES, HEAD_DIM], BF16)
         nc.scalar.dma_start(out=sin_bf[:], in_=sin.rearrange("(t p) d -> p t d", p=P))
+
+        hidden_tiles = []
+        for t in range(TOKEN_TILES):
+            h_rows = hidden_pool.tile([P, DIM], BF16, name="h_rows")
+            nc.sync.dma_start(out=h_rows[:], in_=hidden_rows[t * P : (t + 1) * P, :])
+            hidden_tiles.append(h_rows)
+        for head in range(PREFETCH):
+            load_weights(head)
+
+        ident = const.tile([P, P], F32)
+        make_identity(nc, ident[:])
+        eps_col = const.tile([P, 1], F32)
+        nc.vector.memset(eps_col[:], EPS)
+        warm = const.tile([P, 1], F32)
+        nc.scalar.activation(out=warm[:], in_=eps_col[:], func=ACT.Sqrt)
+
+        def words_to_partitions(rows_words, grouped_words, copies):
+            for pair in range(PASSES // 2):
+                flipped = flipped_pool.tile([P, 2, 2, P], F32, name="flipped")
+                for g2 in range(2):
+                    for u in range(2):
+                        first = (2 * pair + g2) * WORDS + u * P
+                        nc.tensor.transpose(
+                            flipped[:, g2, u, :], rows_words[:, first : first + P], ident[:]
+                        )
+                copies[pair](
+                    out=grouped_words[:, 2 * pair : 2 * pair + 2, :, :],
+                    in_=flipped[:].rearrange("p g u r -> p g r u"),
+                )
+
+        h_grouped = const.tile([P, PASSES * TOKENS * 4], BF16, align_bytes=64)
+        h_grouped_words = (
+            h_grouped[:].bitcast(F32).rearrange("p (g s u) -> p g s u", g=PASSES, u=2)
+        )
+        h_codes = const.tile([P, PASSES * TOKENS], U32, align_bytes=64)
+        h_scales = const.tile([P, PASSES * TOKENS], U8, align_bytes=64)
+        for t in range(TOKEN_TILES):
+            words_to_partitions(
+                hidden_tiles[t][:].bitcast(F32),
+                h_grouped_words[:, :, t * P : (t + 1) * P, :],
+                [nc.scalar.copy, nc.vector.tensor_copy],
+            )
+        for g in range(PASSES):
+            nc.vector.quantize_mx(
+                out=h_codes[:, g * TOKENS : (g + 1) * TOKENS].bitcast(FP8X4),
+                scales=h_scales[:, g * TOKENS : (g + 1) * TOKENS],
+                in_=h_grouped[:, g * TOKENS * 4 : (g + 1) * TOKENS * 4],
+            )
 
         vec_rows = const.tile([P, P], F32)
         nc.vector.tensor_copy(out=vec_rows[:], in_=vec_rows_bf[:])
@@ -106,61 +156,12 @@ def tile_dynamicselfattention_pa_kernel(
             out=sin_signed[:, :, HALF_DIM:HEAD_DIM], in_=sin_bf[:, :, HALF_DIM:HEAD_DIM]
         )
 
-        def words_to_partitions(rows_words, grouped_words):
-            for pair in range(PASSES // 2):
-                flipped = flipped_pool.tile([P, 2, 2, P], F32, name="flipped")
-                for g2 in range(2):
-                    for u in range(2):
-                        first = (2 * pair + g2) * WORDS + u * P
-                        nc.tensor.transpose(
-                            flipped[:, g2, u, :], rows_words[:, first : first + P], ident[:]
-                        )
-                nc.scalar.copy(
-                    out=grouped_words[:, 2 * pair : 2 * pair + 2, :, :],
-                    in_=flipped[:].rearrange("p g u r -> p g r u"),
-                )
-
-        h_grouped = const.tile([P, PASSES * TOKENS * 4], BF16, align_bytes=64)
-        h_grouped_words = (
-            h_grouped[:].bitcast(F32).rearrange("p (g s u) -> p g s u", g=PASSES, u=2)
-        )
-        h_codes = const.tile([P, PASSES * TOKENS], U32, align_bytes=64)
-        h_scales = const.tile([P, PASSES * TOKENS], U8, align_bytes=64)
-        for t in range(TOKEN_TILES):
-            words_to_partitions(
-                hidden_tiles[t][:].bitcast(F32), h_grouped_words[:, :, t * P : (t + 1) * P, :]
-            )
-        for g in range(PASSES):
-            nc.vector.quantize_mx(
-                out=h_codes[:, g * TOKENS : (g + 1) * TOKENS].bitcast(FP8X4),
-                scales=h_scales[:, g * TOKENS : (g + 1) * TOKENS],
-                in_=h_grouped[:, g * TOKENS * 4 : (g + 1) * TOKENS * 4],
-            )
-
-        weight_rows = {}
-        grouped_of = {}
-        codes_of = {}
-        acc_of = {}
-        scaled_of = {}
-        square_sum = {}
-        rotated = {}
-
         def flip(head):
-            load, j = divmod(head, HEADS_PER_LOAD)
-            if j == 0:
-                w_rows = weight_pool.tile([P, HEADS_PER_LOAD, DIM], BF16, name="w_rows")
-                first = load * HEADS_PER_LOAD * P
-                nc.sync.dma_start(
-                    out=w_rows[:],
-                    in_=w_qk[first : first + HEADS_PER_LOAD * P, :].rearrange(
-                        "(j c) k -> c j k", c=P
-                    ),
-                )
-                weight_rows[load] = w_rows
             w_grouped = stage.tile([P, PASSES * P * 4], BF16, name="w_grouped", align_bytes=64)
             words_to_partitions(
-                weight_rows[load][:, j, :].bitcast(F32),
+                weight_rows[head][:].bitcast(F32),
                 w_grouped[:].bitcast(F32).rearrange("p (g c u) -> p g c u", g=PASSES, u=2),
+                [nc.scalar.copy, nc.scalar.copy],
             )
             grouped_of[head] = w_grouped
 
@@ -246,7 +247,7 @@ def tile_dynamicselfattention_pa_kernel(
                 out=rotated[half][:, :, h, :], in0=straight[:], in1=crossed[:], op=ALU.add
             )
 
-        def normalise_and_store(half):
+        def sum_squares(half):
             sums_back = back_pool.tile([P, TOKEN_TILES, HEAD_DIM], F32, name="back")
             for t in range(TOKEN_TILES):
                 nc.tensor.transpose(
@@ -254,26 +255,47 @@ def tile_dynamicselfattention_pa_kernel(
                 )
             total = stage.tile([P, TOKEN_TILES], F32, name="total")
             nc.vector.tensor_reduce(out=total[:], in_=sums_back[:], axis=AXIS.X, op=ALU.add)
+            total_of[half] = total
+
+        def inverse_rms(half):
             rms = stage.tile([P, TOKEN_TILES], F32, name="rms")
             nc.scalar.activation(
-                out=rms[:], in_=total[:], func=ACT.Sqrt, bias=eps_col[:, 0:1], scale=1.0 / DIM
+                out=rms[:],
+                in_=total_of[half][:],
+                func=ACT.Sqrt,
+                bias=eps_col[:, 0:1],
+                scale=1.0 / DIM,
             )
             inv_rms = stage.tile([P, TOKEN_TILES], F32, name="inv_rms")
             nc.vector.reciprocal(out=inv_rms[:], in_=rms[:])
-            for t in range(TOKEN_TILES):
-                row = rotated[half][:, t, :, :].rearrange("p h d -> p (h d)")
-                nc.vector.tensor_scalar(
-                    out=row, in0=row, scalar1=inv_rms[:, t : t + 1], scalar2=None, op0=ALU.mult
-                )
-                nc.sync.dma_start(out=outs[half][t * P : (t + 1) * P, :], in_=row)
+            inv_rms_of[half] = inv_rms
 
-        for step in range(ALL_HEADS + 3):
+        def scale_and_store(half, t):
+            row = rotated[half][:, t, :, :].rearrange("p h d -> p (h d)")
+            nc.vector.tensor_scalar(
+                out=row,
+                in0=row,
+                scalar1=inv_rms_of[half][:, t : t + 1],
+                scalar2=None,
+                op0=ALU.mult,
+            )
+            nc.sync.dma_start(out=outs[half][t * P : (t + 1) * P, :], in_=row)
+
+        for step in range(ALL_HEADS + 3 + TOKEN_TILES):
+            if step + PREFETCH < ALL_HEADS:
+                load_weights(step + PREFETCH)
             if 0 <= step - 1 < ALL_HEADS:
                 quantise(step - 1)
-            if 0 <= step - 3:
+            if 0 <= step - 3 < ALL_HEADS:
                 rotate(step - 3)
-                if (step - 3) % HEADS == HEADS - 1:
-                    normalise_and_store((step - 3) // HEADS)
+            for half in range(2):
+                since = step - 3 - (half * HEADS + HEADS - 1)
+                if since == 0:
+                    sum_squares(half)
+                if since == 1:
+                    inverse_rms(half)
+                if 1 <= since <= TOKEN_TILES:
+                    scale_and_store(half, since - 1)
             if 0 <= step - 2 < ALL_HEADS:
                 bias_gain_square(step - 2)
             if step < ALL_HEADS:

@@ -23,7 +23,7 @@ ALL_HEADS = 2 * HEADS
 K_PASS = 4 * P
 PASSES = DIM // K_PASS
 WORDS = K_PASS // 2
-PREFETCH = 6
+HEADS_PER_LOAD = 4
 EPS = 1e-6
 
 FLOPS = 2 * TOKENS * 2 * DIM * DIM
@@ -42,28 +42,27 @@ def tile_dynamicselfattention_pa_kernel(
     with ExitStack() as ctx:
         const = ctx.enter_context(tc.tile_pool(name="const", bufs=1))
         hidden_pool = ctx.enter_context(tc.tile_pool(name="hidden", bufs=TOKEN_TILES))
-        weight_pool = ctx.enter_context(tc.tile_pool(name="weight", bufs=PREFETCH + 2))
+        weight_pool = ctx.enter_context(tc.tile_pool(name="weight", bufs=3))
         stage = ctx.enter_context(tc.tile_pool(name="stage", bufs=3))
         result_pool = ctx.enter_context(tc.tile_pool(name="result", bufs=2))
-        flipped_pool = ctx.enter_context(tc.psum_pool(name="flipped", bufs=4))
+        flipped_pool = ctx.enter_context(tc.psum_pool(name="flipped", bufs=3))
+        sums_pool = ctx.enter_context(tc.psum_pool(name="sums", bufs=1))
         acc_pool = ctx.enter_context(tc.psum_pool(name="acc", bufs=2))
         back_pool = ctx.enter_context(tc.psum_pool(name="back", bufs=2))
-        ctx.enter_context(tc.manual_schedule())
 
-        weight_rows = {}
-        grouped_of = {}
-        codes_of = {}
-        acc_of = {}
-        scaled_of = {}
-        square_sum = {}
-        rotated = {}
-        inv_rms_of = {}
-        total_of = {}
+        ident = const.tile([P, P], F32)
+        make_identity(nc, ident[:])
 
-        def load_weights(head):
-            w_rows = weight_pool.tile([P, DIM], BF16, name="w_rows")
-            nc.sync.dma_start(out=w_rows[:], in_=w_qk[head * P : (head + 1) * P, :])
-            weight_rows[head] = w_rows
+        eps_col = const.tile([P, 1], F32)
+        nc.vector.memset(eps_col[:], EPS)
+        warm = const.tile([P, 1], F32)
+        nc.scalar.activation(out=warm[:], in_=eps_col[:], func=ACT.Sqrt)
+
+        hidden_tiles = []
+        for t in range(TOKEN_TILES):
+            h_rows = hidden_pool.tile([P, DIM], BF16, name="h_rows")
+            nc.sync.dma_start(out=h_rows[:], in_=hidden_rows[t * P : (t + 1) * P, :])
+            hidden_tiles.append(h_rows)
 
         vec_rows_bf = const.tile([P, P], BF16)
         nc.vector.memset(vec_rows_bf[:], 0.0)
@@ -82,54 +81,6 @@ def tile_dynamicselfattention_pa_kernel(
         nc.scalar.dma_start(out=cos_bf[:], in_=cos.rearrange("(t p) d -> p t d", p=P))
         sin_bf = const.tile([P, TOKEN_TILES, HEAD_DIM], BF16)
         nc.scalar.dma_start(out=sin_bf[:], in_=sin.rearrange("(t p) d -> p t d", p=P))
-
-        hidden_tiles = []
-        for t in range(TOKEN_TILES):
-            h_rows = hidden_pool.tile([P, DIM], BF16, name="h_rows")
-            nc.sync.dma_start(out=h_rows[:], in_=hidden_rows[t * P : (t + 1) * P, :])
-            hidden_tiles.append(h_rows)
-        for head in range(PREFETCH):
-            load_weights(head)
-
-        ident = const.tile([P, P], F32)
-        make_identity(nc, ident[:])
-        eps_col = const.tile([P, 1], F32)
-        nc.vector.memset(eps_col[:], EPS)
-        warm = const.tile([P, 1], F32)
-        nc.scalar.activation(out=warm[:], in_=eps_col[:], func=ACT.Sqrt)
-
-        def words_to_partitions(rows_words, grouped_words, copies):
-            for pair in range(PASSES // 2):
-                flipped = flipped_pool.tile([P, 2, 2, P], F32, name="flipped")
-                for g2 in range(2):
-                    for u in range(2):
-                        first = (2 * pair + g2) * WORDS + u * P
-                        nc.tensor.transpose(
-                            flipped[:, g2, u, :], rows_words[:, first : first + P], ident[:]
-                        )
-                copies[pair](
-                    out=grouped_words[:, 2 * pair : 2 * pair + 2, :, :],
-                    in_=flipped[:].rearrange("p g u r -> p g r u"),
-                )
-
-        h_grouped = const.tile([P, PASSES * TOKENS * 4], BF16, align_bytes=64)
-        h_grouped_words = (
-            h_grouped[:].bitcast(F32).rearrange("p (g s u) -> p g s u", g=PASSES, u=2)
-        )
-        h_codes = const.tile([P, PASSES * TOKENS], U32, align_bytes=64)
-        h_scales = const.tile([P, PASSES * TOKENS], U8, align_bytes=64)
-        for t in range(TOKEN_TILES):
-            words_to_partitions(
-                hidden_tiles[t][:].bitcast(F32),
-                h_grouped_words[:, :, t * P : (t + 1) * P, :],
-                [nc.scalar.copy, nc.vector.tensor_copy],
-            )
-        for g in range(PASSES):
-            nc.vector.quantize_mx(
-                out=h_codes[:, g * TOKENS : (g + 1) * TOKENS].bitcast(FP8X4),
-                scales=h_scales[:, g * TOKENS : (g + 1) * TOKENS],
-                in_=h_grouped[:, g * TOKENS * 4 : (g + 1) * TOKENS * 4],
-            )
 
         vec_rows = const.tile([P, P], F32)
         nc.vector.tensor_copy(out=vec_rows[:], in_=vec_rows_bf[:])
@@ -156,12 +107,61 @@ def tile_dynamicselfattention_pa_kernel(
             out=sin_signed[:, :, HALF_DIM:HEAD_DIM], in_=sin_bf[:, :, HALF_DIM:HEAD_DIM]
         )
 
+        def words_to_partitions(rows_words, grouped_words):
+            for pair in range(PASSES // 2):
+                flipped = flipped_pool.tile([P, 2, 2, P], F32, name="flipped")
+                for g2 in range(2):
+                    for u in range(2):
+                        first = (2 * pair + g2) * WORDS + u * P
+                        nc.tensor.transpose(
+                            flipped[:, g2, u, :], rows_words[:, first : first + P], ident[:]
+                        )
+                nc.scalar.copy(
+                    out=grouped_words[:, 2 * pair : 2 * pair + 2, :, :],
+                    in_=flipped[:].rearrange("p g u r -> p g r u"),
+                )
+
+        h_grouped = const.tile([P, PASSES * TOKENS * 4], BF16, align_bytes=64)
+        h_grouped_words = (
+            h_grouped[:].bitcast(F32).rearrange("p (g s u) -> p g s u", g=PASSES, u=2)
+        )
+        h_codes = const.tile([P, PASSES * TOKENS], U32, align_bytes=64)
+        h_scales = const.tile([P, PASSES * TOKENS], U8, align_bytes=64)
+        for t in range(TOKEN_TILES):
+            words_to_partitions(
+                hidden_tiles[t][:].bitcast(F32), h_grouped_words[:, :, t * P : (t + 1) * P, :]
+            )
+        for g in range(PASSES):
+            nc.vector.quantize_mx(
+                out=h_codes[:, g * TOKENS : (g + 1) * TOKENS].bitcast(FP8X4),
+                scales=h_scales[:, g * TOKENS : (g + 1) * TOKENS],
+                in_=h_grouped[:, g * TOKENS * 4 : (g + 1) * TOKENS * 4],
+            )
+
+        weight_rows = {}
+        grouped_of = {}
+        codes_of = {}
+        acc_of = {}
+        scaled_of = {}
+        square_sum = {}
+        rotated = {}
+
         def flip(head):
+            load, j = divmod(head, HEADS_PER_LOAD)
+            if j == 0:
+                w_rows = weight_pool.tile([P, HEADS_PER_LOAD, DIM], BF16, name="w_rows")
+                first = load * HEADS_PER_LOAD * P
+                nc.sync.dma_start(
+                    out=w_rows[:],
+                    in_=w_qk[first : first + HEADS_PER_LOAD * P, :].rearrange(
+                        "(j c) k -> c j k", c=P
+                    ),
+                )
+                weight_rows[load] = w_rows
             w_grouped = stage.tile([P, PASSES * P * 4], BF16, name="w_grouped", align_bytes=64)
             words_to_partitions(
-                weight_rows[head][:].bitcast(F32),
+                weight_rows[load][:, j, :].bitcast(F32),
                 w_grouped[:].bitcast(F32).rearrange("p (g c u) -> p g c u", g=PASSES, u=2),
-                [nc.scalar.copy, nc.scalar.copy],
             )
             grouped_of[head] = w_grouped
 
@@ -200,11 +200,7 @@ def tile_dynamicselfattention_pa_kernel(
                 scale=gain_col[:, head : head + 1],
             )
             scaled_of[head] = scaled
-            if h == 0:
-                square = result_pool.tile([P, TOKENS], F32, name="square_sum")
-                square_sum[half] = square
-            else:
-                square = stage.tile([P, TOKENS], F32, name="square")
+            square = stage.tile([P, TOKENS], F32, name="square")
             nc.scalar.activation(
                 out=square[:],
                 in_=acc[:],
@@ -212,9 +208,16 @@ def tile_dynamicselfattention_pa_kernel(
                 bias=bias_col[:, head : head + 1],
                 scale=1.0,
             )
-            if h > 0:
-                nc.gpsimd.tensor_tensor(
-                    out=square_sum[half][:], in0=square_sum[half][:], in1=square[:], op=ALU.add
+            if h == 0:
+                square_sum[half] = sums_pool.tile([P, TOKEN_TILES, HEAD_DIM], F32, name="sums")
+            for t in range(TOKEN_TILES):
+                nc.tensor.matmul(
+                    out=square_sum[half][:, t, :],
+                    lhsT=square[:, t * P : (t + 1) * P],
+                    rhs=ident[:],
+                    is_transpose=True,
+                    start=(h == 0 and t == 0),
+                    stop=(h == HEADS - 1 and t == TOKEN_TILES - 1),
                 )
 
         def rotate(head):
@@ -247,55 +250,31 @@ def tile_dynamicselfattention_pa_kernel(
                 out=rotated[half][:, :, h, :], in0=straight[:], in1=crossed[:], op=ALU.add
             )
 
-        def sum_squares(half):
-            sums_back = back_pool.tile([P, TOKEN_TILES, HEAD_DIM], F32, name="back")
-            for t in range(TOKEN_TILES):
-                nc.tensor.transpose(
-                    sums_back[:, t, :], square_sum[half][:, t * P : (t + 1) * P], ident[:]
-                )
+        def normalise_and_store(half):
             total = stage.tile([P, TOKEN_TILES], F32, name="total")
-            nc.vector.tensor_reduce(out=total[:], in_=sums_back[:], axis=AXIS.X, op=ALU.add)
-            total_of[half] = total
-
-        def inverse_rms(half):
+            nc.vector.tensor_reduce(
+                out=total[:], in_=square_sum[half][:], axis=AXIS.X, op=ALU.add
+            )
             rms = stage.tile([P, TOKEN_TILES], F32, name="rms")
             nc.scalar.activation(
-                out=rms[:],
-                in_=total_of[half][:],
-                func=ACT.Sqrt,
-                bias=eps_col[:, 0:1],
-                scale=1.0 / DIM,
+                out=rms[:], in_=total[:], func=ACT.Sqrt, bias=eps_col[:, 0:1], scale=1.0 / DIM
             )
             inv_rms = stage.tile([P, TOKEN_TILES], F32, name="inv_rms")
             nc.vector.reciprocal(out=inv_rms[:], in_=rms[:])
-            inv_rms_of[half] = inv_rms
+            for t in range(TOKEN_TILES):
+                row = rotated[half][:, t, :, :].rearrange("p h d -> p (h d)")
+                nc.vector.tensor_scalar(
+                    out=row, in0=row, scalar1=inv_rms[:, t : t + 1], scalar2=None, op0=ALU.mult
+                )
+                nc.sync.dma_start(out=outs[half][t * P : (t + 1) * P, :], in_=row)
 
-        def scale_and_store(half, t):
-            row = rotated[half][:, t, :, :].rearrange("p h d -> p (h d)")
-            nc.vector.tensor_scalar(
-                out=row,
-                in0=row,
-                scalar1=inv_rms_of[half][:, t : t + 1],
-                scalar2=None,
-                op0=ALU.mult,
-            )
-            nc.sync.dma_start(out=outs[half][t * P : (t + 1) * P, :], in_=row)
-
-        for step in range(ALL_HEADS + 3 + TOKEN_TILES):
-            if step + PREFETCH < ALL_HEADS:
-                load_weights(step + PREFETCH)
+        for step in range(ALL_HEADS + 3):
             if 0 <= step - 1 < ALL_HEADS:
                 quantise(step - 1)
-            if 0 <= step - 3 < ALL_HEADS:
+            if 0 <= step - 3:
                 rotate(step - 3)
-            for half in range(2):
-                since = step - 3 - (half * HEADS + HEADS - 1)
-                if since == 0:
-                    sum_squares(half)
-                if since == 1:
-                    inverse_rms(half)
-                if 1 <= since <= TOKEN_TILES:
-                    scale_and_store(half, since - 1)
+                if (step - 3) % HEADS == HEADS - 1:
+                    normalise_and_store((step - 3) // HEADS)
             if 0 <= step - 2 < ALL_HEADS:
                 bias_gain_square(step - 2)
             if step < ALL_HEADS:

@@ -23,7 +23,7 @@ ALL_HEADS = 2 * HEADS
 K_PASS = 4 * P
 PASSES = DIM // K_PASS
 WORDS = K_PASS // 2
-HEADS_PER_LOAD = 4
+PREFETCH = 6
 EPS = 1e-6
 
 FLOPS = 2 * TOKENS * 2 * DIM * DIM
@@ -42,27 +42,29 @@ def tile_dynamicselfattention_pa_kernel(
     with ExitStack() as ctx:
         const = ctx.enter_context(tc.tile_pool(name="const", bufs=1))
         hidden_pool = ctx.enter_context(tc.tile_pool(name="hidden", bufs=TOKEN_TILES))
-        weight_pool = ctx.enter_context(tc.tile_pool(name="weight", bufs=3))
+        weight_pool = ctx.enter_context(tc.tile_pool(name="weight", bufs=PREFETCH + 2))
         stage = ctx.enter_context(tc.tile_pool(name="stage", bufs=3))
         result_pool = ctx.enter_context(tc.tile_pool(name="result", bufs=2))
-        flipped_pool = ctx.enter_context(tc.psum_pool(name="flipped", bufs=3))
-        sums_pool = ctx.enter_context(tc.psum_pool(name="sums", bufs=1))
+        flipped_pool = ctx.enter_context(tc.psum_pool(name="flipped", bufs=4))
         acc_pool = ctx.enter_context(tc.psum_pool(name="acc", bufs=2))
         back_pool = ctx.enter_context(tc.psum_pool(name="back", bufs=2))
+        ctx.enter_context(tc.manual_schedule())
 
-        ident = const.tile([P, P], F32)
-        make_identity(nc, ident[:])
+        weight_rows = {}
+        flipped_of = {}
+        grouped_of = {}
+        codes_of = {}
+        acc_of = {}
+        scaled_of = {}
+        square_sum = {}
+        rotated = {}
+        inv_rms_of = {}
+        total_of = {}
 
-        eps_col = const.tile([P, 1], F32)
-        nc.vector.memset(eps_col[:], EPS)
-        warm = const.tile([P, 1], F32)
-        nc.scalar.activation(out=warm[:], in_=eps_col[:], func=ACT.Sqrt)
-
-        hidden_tiles = []
-        for t in range(TOKEN_TILES):
-            h_rows = hidden_pool.tile([P, DIM], BF16, name="h_rows")
-            nc.sync.dma_start(out=h_rows[:], in_=hidden_rows[t * P : (t + 1) * P, :])
-            hidden_tiles.append(h_rows)
+        def load_weights(head):
+            w_rows = weight_pool.tile([P, DIM], BF16, name="w_rows")
+            nc.sync.dma_start(out=w_rows[:], in_=w_qk[head * P : (head + 1) * P, :])
+            weight_rows[head] = w_rows
 
         vec_rows_bf = const.tile([P, P], BF16)
         nc.vector.memset(vec_rows_bf[:], 0.0)
@@ -81,6 +83,54 @@ def tile_dynamicselfattention_pa_kernel(
         nc.scalar.dma_start(out=cos_bf[:], in_=cos.rearrange("(t p) d -> p t d", p=P))
         sin_bf = const.tile([P, TOKEN_TILES, HEAD_DIM], BF16)
         nc.scalar.dma_start(out=sin_bf[:], in_=sin.rearrange("(t p) d -> p t d", p=P))
+
+        hidden_tiles = []
+        for t in range(TOKEN_TILES):
+            h_rows = hidden_pool.tile([P, DIM], BF16, name="h_rows")
+            nc.sync.dma_start(out=h_rows[:], in_=hidden_rows[t * P : (t + 1) * P, :])
+            hidden_tiles.append(h_rows)
+        for head in range(PREFETCH):
+            load_weights(head)
+
+        ident = const.tile([P, P], F32)
+        make_identity(nc, ident[:])
+        eps_col = const.tile([P, 1], F32)
+        nc.vector.memset(eps_col[:], EPS)
+        warm = const.tile([P, 1], F32)
+        nc.scalar.activation(out=warm[:], in_=eps_col[:], func=ACT.Sqrt)
+
+        def transpose_words(rows_words, pair):
+            flipped = flipped_pool.tile([P, 2, 2, P], F32, name="flipped")
+            for g2 in range(2):
+                for u in range(2):
+                    first = (2 * pair + g2) * WORDS + u * P
+                    nc.tensor.transpose(
+                        flipped[:, g2, u, :], rows_words[:, first : first + P], ident[:]
+                    )
+            return flipped
+
+        def regroup(flipped, grouped_words, pair, copy):
+            copy(
+                out=grouped_words[:, 2 * pair : 2 * pair + 2, :, :],
+                in_=flipped[:].rearrange("p g u r -> p g r u"),
+            )
+
+        h_grouped = const.tile([P, PASSES * TOKENS * 4], BF16, align_bytes=64)
+        h_grouped_words = (
+            h_grouped[:].bitcast(F32).rearrange("p (g s u) -> p g s u", g=PASSES, u=2)
+        )
+        h_codes = const.tile([P, PASSES * TOKENS], U32, align_bytes=64)
+        h_scales = const.tile([P, PASSES * TOKENS], U8, align_bytes=64)
+        for t in range(TOKEN_TILES):
+            for pair, copy in enumerate([nc.scalar.copy, nc.vector.tensor_copy]):
+                flipped = transpose_words(hidden_tiles[t][:].bitcast(F32), pair)
+                regroup(flipped, h_grouped_words[:, :, t * P : (t + 1) * P, :], pair, copy)
+        for g in range(PASSES):
+            nc.vector.quantize_mx(
+                out=h_codes[:, g * TOKENS : (g + 1) * TOKENS].bitcast(FP8X4),
+                scales=h_scales[:, g * TOKENS : (g + 1) * TOKENS],
+                in_=h_grouped[:, g * TOKENS * 4 : (g + 1) * TOKENS * 4],
+            )
 
         vec_rows = const.tile([P, P], F32)
         nc.vector.tensor_copy(out=vec_rows[:], in_=vec_rows_bf[:])
@@ -107,62 +157,16 @@ def tile_dynamicselfattention_pa_kernel(
             out=sin_signed[:, :, HALF_DIM:HEAD_DIM], in_=sin_bf[:, :, HALF_DIM:HEAD_DIM]
         )
 
-        def words_to_partitions(rows_words, grouped_words):
-            for pair in range(PASSES // 2):
-                flipped = flipped_pool.tile([P, 2, 2, P], F32, name="flipped")
-                for g2 in range(2):
-                    for u in range(2):
-                        first = (2 * pair + g2) * WORDS + u * P
-                        nc.tensor.transpose(
-                            flipped[:, g2, u, :], rows_words[:, first : first + P], ident[:]
-                        )
-                nc.scalar.copy(
-                    out=grouped_words[:, 2 * pair : 2 * pair + 2, :, :],
-                    in_=flipped[:].rearrange("p g u r -> p g r u"),
-                )
+        def flip(head, pair):
+            flipped_of[(head, pair)] = transpose_words(weight_rows[head][:].bitcast(F32), pair)
 
-        h_grouped = const.tile([P, PASSES * TOKENS * 4], BF16, align_bytes=64)
-        h_grouped_words = (
-            h_grouped[:].bitcast(F32).rearrange("p (g s u) -> p g s u", g=PASSES, u=2)
-        )
-        h_codes = const.tile([P, PASSES * TOKENS], U32, align_bytes=64)
-        h_scales = const.tile([P, PASSES * TOKENS], U8, align_bytes=64)
-        for t in range(TOKEN_TILES):
-            words_to_partitions(
-                hidden_tiles[t][:].bitcast(F32), h_grouped_words[:, :, t * P : (t + 1) * P, :]
-            )
-        for g in range(PASSES):
-            nc.vector.quantize_mx(
-                out=h_codes[:, g * TOKENS : (g + 1) * TOKENS].bitcast(FP8X4),
-                scales=h_scales[:, g * TOKENS : (g + 1) * TOKENS],
-                in_=h_grouped[:, g * TOKENS * 4 : (g + 1) * TOKENS * 4],
-            )
-
-        weight_rows = {}
-        grouped_of = {}
-        codes_of = {}
-        acc_of = {}
-        scaled_of = {}
-        square_sum = {}
-        rotated = {}
-
-        def flip(head):
-            load, j = divmod(head, HEADS_PER_LOAD)
-            if j == 0:
-                w_rows = weight_pool.tile([P, HEADS_PER_LOAD, DIM], BF16, name="w_rows")
-                first = load * HEADS_PER_LOAD * P
-                nc.sync.dma_start(
-                    out=w_rows[:],
-                    in_=w_qk[first : first + HEADS_PER_LOAD * P, :].rearrange(
-                        "(j c) k -> c j k", c=P
-                    ),
-                )
-                weight_rows[load] = w_rows
+        def regroup_weights(head):
             w_grouped = stage.tile([P, PASSES * P * 4], BF16, name="w_grouped", align_bytes=64)
-            words_to_partitions(
-                weight_rows[load][:, j, :].bitcast(F32),
-                w_grouped[:].bitcast(F32).rearrange("p (g c u) -> p g c u", g=PASSES, u=2),
+            w_grouped_words = (
+                w_grouped[:].bitcast(F32).rearrange("p (g c u) -> p g c u", g=PASSES, u=2)
             )
+            for pair in range(PASSES // 2):
+                regroup(flipped_of[(head, pair)], w_grouped_words, pair, nc.scalar.copy)
             grouped_of[head] = w_grouped
 
         def quantise(head):
@@ -173,12 +177,13 @@ def tile_dynamicselfattention_pa_kernel(
             )
             codes_of[head] = (w_codes, w_scales)
 
-        def multiply(head):
+        def multiply(head, pair):
             w_codes, w_scales = codes_of[head]
-            acc = acc_pool.tile([P, TOKENS], F32, name="acc")
-            for g in range(PASSES):
+            if pair == 0:
+                acc_of[head] = acc_pool.tile([P, TOKENS], F32, name="acc")
+            for g in range(2 * pair, 2 * pair + 2):
                 nc.tensor.matmul_mx(
-                    out=acc[:],
+                    out=acc_of[head][:],
                     lhsT=w_codes[:, g * P : (g + 1) * P].bitcast(FP8X4),
                     lhsT_scale=w_scales[:, g * P : (g + 1) * P],
                     rhs=h_codes[:, g * TOKENS : (g + 1) * TOKENS].bitcast(FP8X4),
@@ -186,7 +191,6 @@ def tile_dynamicselfattention_pa_kernel(
                     start=(g == 0),
                     stop=(g == PASSES - 1),
                 )
-            acc_of[head] = acc
 
         def bias_gain_square(head):
             half, h = divmod(head, HEADS)
@@ -200,7 +204,11 @@ def tile_dynamicselfattention_pa_kernel(
                 scale=gain_col[:, head : head + 1],
             )
             scaled_of[head] = scaled
-            square = stage.tile([P, TOKENS], F32, name="square")
+            if h == 0:
+                square = result_pool.tile([P, TOKENS], F32, name="square_sum")
+                square_sum[half] = square
+            else:
+                square = stage.tile([P, TOKENS], F32, name="square")
             nc.scalar.activation(
                 out=square[:],
                 in_=acc[:],
@@ -208,16 +216,9 @@ def tile_dynamicselfattention_pa_kernel(
                 bias=bias_col[:, head : head + 1],
                 scale=1.0,
             )
-            if h == 0:
-                square_sum[half] = sums_pool.tile([P, TOKEN_TILES, HEAD_DIM], F32, name="sums")
-            for t in range(TOKEN_TILES):
-                nc.tensor.matmul(
-                    out=square_sum[half][:, t, :],
-                    lhsT=square[:, t * P : (t + 1) * P],
-                    rhs=ident[:],
-                    is_transpose=True,
-                    start=(h == 0 and t == 0),
-                    stop=(h == HEADS - 1 and t == TOKEN_TILES - 1),
+            if h > 0:
+                nc.gpsimd.tensor_tensor(
+                    out=square_sum[half][:], in0=square_sum[half][:], in1=square[:], op=ALU.add
                 )
 
         def rotate(head):
@@ -250,34 +251,62 @@ def tile_dynamicselfattention_pa_kernel(
                 out=rotated[half][:, :, h, :], in0=straight[:], in1=crossed[:], op=ALU.add
             )
 
-        def normalise_and_store(half):
+        def sum_squares(half):
+            sums_back = back_pool.tile([P, TOKEN_TILES, HEAD_DIM], F32, name="back")
+            for t in range(TOKEN_TILES):
+                nc.tensor.transpose(
+                    sums_back[:, t, :], square_sum[half][:, t * P : (t + 1) * P], ident[:]
+                )
             total = stage.tile([P, TOKEN_TILES], F32, name="total")
-            nc.vector.tensor_reduce(
-                out=total[:], in_=square_sum[half][:], axis=AXIS.X, op=ALU.add
-            )
+            nc.vector.tensor_reduce(out=total[:], in_=sums_back[:], axis=AXIS.X, op=ALU.add)
+            total_of[half] = total
+
+        def inverse_rms(half):
             rms = stage.tile([P, TOKEN_TILES], F32, name="rms")
             nc.scalar.activation(
-                out=rms[:], in_=total[:], func=ACT.Sqrt, bias=eps_col[:, 0:1], scale=1.0 / DIM
+                out=rms[:],
+                in_=total_of[half][:],
+                func=ACT.Sqrt,
+                bias=eps_col[:, 0:1],
+                scale=1.0 / DIM,
             )
             inv_rms = stage.tile([P, TOKEN_TILES], F32, name="inv_rms")
             nc.vector.reciprocal(out=inv_rms[:], in_=rms[:])
-            for t in range(TOKEN_TILES):
-                row = rotated[half][:, t, :, :].rearrange("p h d -> p (h d)")
-                nc.vector.tensor_scalar(
-                    out=row, in0=row, scalar1=inv_rms[:, t : t + 1], scalar2=None, op0=ALU.mult
-                )
-                nc.sync.dma_start(out=outs[half][t * P : (t + 1) * P, :], in_=row)
+            inv_rms_of[half] = inv_rms
 
-        for step in range(ALL_HEADS + 3):
-            if 0 <= step - 1 < ALL_HEADS:
-                quantise(step - 1)
-            if 0 <= step - 3:
-                rotate(step - 3)
-                if (step - 3) % HEADS == HEADS - 1:
-                    normalise_and_store((step - 3) // HEADS)
+        def scale_and_store(half, t):
+            row = rotated[half][:, t, :, :].rearrange("p h d -> p (h d)")
+            nc.vector.tensor_scalar(
+                out=row,
+                in0=row,
+                scalar1=inv_rms_of[half][:, t : t + 1],
+                scalar2=None,
+                op0=ALU.mult,
+            )
+            nc.sync.dma_start(out=outs[half][t * P : (t + 1) * P, :], in_=row)
+
+        LAST_STAGE = 5
+        for step in range(ALL_HEADS + LAST_STAGE + TOKEN_TILES):
+            if step + PREFETCH < ALL_HEADS:
+                load_weights(step + PREFETCH)
             if 0 <= step - 2 < ALL_HEADS:
-                bias_gain_square(step - 2)
-            if step < ALL_HEADS:
-                flip(step)
+                quantise(step - 2)
+            if 0 <= step - LAST_STAGE < ALL_HEADS:
+                rotate(step - LAST_STAGE)
+            for half in range(2):
+                since = step - LAST_STAGE - (half * HEADS + HEADS - 1)
+                if since == 0:
+                    sum_squares(half)
+                if since == 1:
+                    inverse_rms(half)
+                if 1 <= since <= TOKEN_TILES:
+                    scale_and_store(half, since - 1)
+            if 0 <= step - 4 < ALL_HEADS:
+                bias_gain_square(step - 4)
             if 0 <= step - 1 < ALL_HEADS:
-                multiply(step - 1)
+                regroup_weights(step - 1)
+            for pair in range(PASSES // 2):
+                if step < ALL_HEADS:
+                    flip(step, pair)
+                if 0 <= step - 3 < ALL_HEADS:
+                    multiply(step - 3, pair)

from contextlib import ExitStack

import concourse.mybir as mybir
from concourse.masks import make_identity

F32 = mybir.dt.float32
BF16 = mybir.dt.bfloat16
U32 = mybir.dt.uint32
U8 = mybir.dt.uint8
FP8X4 = mybir.dt.float8_e4m3fn_x4
ACT = mybir.ActivationFunctionType
ALU = mybir.AluOpType
AXIS = mybir.AxisListType

P = 128
TOKENS = 512
TOKEN_TILES = TOKENS // P
DIM = 2048
HEAD_DIM = 128
HALF_DIM = HEAD_DIM // 2
HEADS = DIM // HEAD_DIM
ALL_HEADS = 2 * HEADS
K_PASS = 4 * P
PASSES = DIM // K_PASS
WORDS = K_PASS // 2
PREFETCH = 6
EPS = 1e-6

FLOPS = 2 * TOKENS * 2 * DIM * DIM


def tile_dynamicselfattention_pa_kernel(
    tc, hidden_states, cos, sin, w_qk, b_qk, g_q, g_k, out_0, out_1
):
    nc = tc.nc
    hidden_rows = hidden_states.flatten_outer_dims()
    outs = [
        out_0.rearrange("b s h d -> (b s) (h d)"),
        out_1.rearrange("b s h d -> (b s) (h d)"),
    ]

    with ExitStack() as ctx:
        const = ctx.enter_context(tc.tile_pool(name="const", bufs=1))
        hidden_pool = ctx.enter_context(tc.tile_pool(name="hidden", bufs=TOKEN_TILES))
        weight_pool = ctx.enter_context(tc.tile_pool(name="weight", bufs=PREFETCH + 2))
        stage = ctx.enter_context(tc.tile_pool(name="stage", bufs=3))
        result_pool = ctx.enter_context(tc.tile_pool(name="result", bufs=2))
        flipped_pool = ctx.enter_context(tc.psum_pool(name="flipped", bufs=4))
        acc_pool = ctx.enter_context(tc.psum_pool(name="acc", bufs=2))
        back_pool = ctx.enter_context(tc.psum_pool(name="back", bufs=2))
        ctx.enter_context(tc.manual_schedule())

        weight_rows = {}
        flipped_of = {}
        grouped_of = {}
        codes_of = {}
        acc_of = {}
        scaled_of = {}
        square_sum = {}
        rotated = {}
        inv_rms_of = {}
        total_of = {}

        def load_weights(head):
            w_rows = weight_pool.tile([P, DIM], BF16, name="w_rows")
            nc.sync.dma_start(out=w_rows[:], in_=w_qk[head * P : (head + 1) * P, :])
            weight_rows[head] = w_rows

        vec_rows_bf = const.tile([P, P], BF16)
        nc.vector.memset(vec_rows_bf[:], 0.0)
        nc.scalar.dma_start(
            out=vec_rows_bf[0:ALL_HEADS, :], in_=b_qk.rearrange("(h d) -> h d", d=HEAD_DIM)
        )
        nc.scalar.dma_start(
            out=vec_rows_bf[ALL_HEADS : ALL_HEADS + HEADS, :],
            in_=g_q.rearrange("(h d) -> h d", d=HEAD_DIM),
        )
        nc.scalar.dma_start(
            out=vec_rows_bf[ALL_HEADS + HEADS : 2 * ALL_HEADS, :],
            in_=g_k.rearrange("(h d) -> h d", d=HEAD_DIM),
        )
        cos_bf = const.tile([P, TOKEN_TILES, HEAD_DIM], BF16)
        nc.scalar.dma_start(out=cos_bf[:], in_=cos.rearrange("(t p) d -> p t d", p=P))
        sin_bf = const.tile([P, TOKEN_TILES, HEAD_DIM], BF16)
        nc.scalar.dma_start(out=sin_bf[:], in_=sin.rearrange("(t p) d -> p t d", p=P))

        hidden_tiles = []
        for t in range(TOKEN_TILES):
            h_rows = hidden_pool.tile([P, DIM], BF16, name="h_rows")
            nc.sync.dma_start(out=h_rows[:], in_=hidden_rows[t * P : (t + 1) * P, :])
            hidden_tiles.append(h_rows)
        for head in range(PREFETCH):
            load_weights(head)

        ident = const.tile([P, P], F32)
        make_identity(nc, ident[:])
        eps_col = const.tile([P, 1], F32)
        nc.vector.memset(eps_col[:], EPS)
        warm = const.tile([P, 1], F32)
        nc.scalar.activation(out=warm[:], in_=eps_col[:], func=ACT.Sqrt)

        def transpose_words(rows_words, pair):
            flipped = flipped_pool.tile([P, 2, 2, P], F32, name="flipped")
            for g2 in range(2):
                for u in range(2):
                    first = (2 * pair + g2) * WORDS + u * P
                    nc.tensor.transpose(
                        flipped[:, g2, u, :], rows_words[:, first : first + P], ident[:]
                    )
            return flipped

        def regroup(flipped, grouped_words, pair, copy):
            copy(
                out=grouped_words[:, 2 * pair : 2 * pair + 2, :, :],
                in_=flipped[:].rearrange("p g u r -> p g r u"),
            )

        h_grouped = const.tile([P, PASSES * TOKENS * 4], BF16, align_bytes=64)
        h_grouped_words = (
            h_grouped[:].bitcast(F32).rearrange("p (g s u) -> p g s u", g=PASSES, u=2)
        )
        h_codes = const.tile([P, PASSES * TOKENS], U32, align_bytes=64)
        h_scales = const.tile([P, PASSES * TOKENS], U8, align_bytes=64)
        for t in range(TOKEN_TILES):
            for pair, copy in enumerate([nc.scalar.copy, nc.vector.tensor_copy]):
                flipped = transpose_words(hidden_tiles[t][:].bitcast(F32), pair)
                regroup(flipped, h_grouped_words[:, :, t * P : (t + 1) * P, :], pair, copy)
        for g in range(PASSES):
            nc.vector.quantize_mx(
                out=h_codes[:, g * TOKENS : (g + 1) * TOKENS].bitcast(FP8X4),
                scales=h_scales[:, g * TOKENS : (g + 1) * TOKENS],
                in_=h_grouped[:, g * TOKENS * 4 : (g + 1) * TOKENS * 4],
            )

        vec_rows = const.tile([P, P], F32)
        nc.vector.tensor_copy(out=vec_rows[:], in_=vec_rows_bf[:])
        vec_cols_ps = back_pool.tile([P, TOKEN_TILES, HEAD_DIM], F32, tag="back")
        nc.tensor.transpose(vec_cols_ps[:, 0, :], vec_rows[:], ident[:])
        vec_cols = const.tile([P, P], F32)
        nc.vector.tensor_copy(out=vec_cols[:], in_=vec_cols_ps[:, 0, :])
        bias_col = vec_cols[:, 0:ALL_HEADS]
        gain_col = vec_cols[:, ALL_HEADS : 2 * ALL_HEADS]
        gain_bias_col = const.tile([P, ALL_HEADS], F32)
        nc.vector.tensor_tensor(out=gain_bias_col[:], in0=bias_col, in1=gain_col, op=ALU.mult)

        cos_f = const.tile([P, TOKEN_TILES, HEAD_DIM], F32)
        nc.vector.tensor_copy(out=cos_f[:], in_=cos_bf[:])
        sin_signed = const.tile([P, TOKEN_TILES, HEAD_DIM], F32)
        nc.vector.tensor_scalar(
            out=sin_signed[:, :, 0:HALF_DIM],
            in0=sin_bf[:, :, 0:HALF_DIM],
            scalar1=-1.0,
            scalar2=None,
            op0=ALU.mult,
        )
        nc.vector.tensor_copy(
            out=sin_signed[:, :, HALF_DIM:HEAD_DIM], in_=sin_bf[:, :, HALF_DIM:HEAD_DIM]
        )

        def flip(head, pair):
            flipped_of[(head, pair)] = transpose_words(weight_rows[head][:].bitcast(F32), pair)

        def regroup_weights(head):
            w_grouped = stage.tile([P, PASSES * P * 4], BF16, name="w_grouped", align_bytes=64)
            w_grouped_words = (
                w_grouped[:].bitcast(F32).rearrange("p (g c u) -> p g c u", g=PASSES, u=2)
            )
            for pair in range(PASSES // 2):
                regroup(flipped_of[(head, pair)], w_grouped_words, pair, nc.scalar.copy)
            grouped_of[head] = w_grouped

        def quantise(head):
            w_codes = stage.tile([P, PASSES * P], U32, name="w_codes", align_bytes=64)
            w_scales = stage.tile([P, PASSES * P], U8, name="w_scales", align_bytes=64)
            nc.vector.quantize_mx(
                out=w_codes[:].bitcast(FP8X4), scales=w_scales[:], in_=grouped_of[head][:]
            )
            codes_of[head] = (w_codes, w_scales)

        def multiply(head, pair):
            w_codes, w_scales = codes_of[head]
            if pair == 0:
                acc_of[head] = acc_pool.tile([P, TOKENS], F32, name="acc")
            for g in range(2 * pair, 2 * pair + 2):
                nc.tensor.matmul_mx(
                    out=acc_of[head][:],
                    lhsT=w_codes[:, g * P : (g + 1) * P].bitcast(FP8X4),
                    lhsT_scale=w_scales[:, g * P : (g + 1) * P],
                    rhs=h_codes[:, g * TOKENS : (g + 1) * TOKENS].bitcast(FP8X4),
                    rhs_scale=h_scales[:, g * TOKENS : (g + 1) * TOKENS],
                    start=(g == 0),
                    stop=(g == PASSES - 1),
                )

        def bias_gain_square(head):
            half, h = divmod(head, HEADS)
            acc = acc_of[head]
            scaled = stage.tile([P, TOKENS], F32, name="scaled")
            nc.scalar.activation(
                out=scaled[:],
                in_=acc[:],
                func=ACT.Identity,
                bias=gain_bias_col[:, head : head + 1],
                scale=gain_col[:, head : head + 1],
            )
            scaled_of[head] = scaled
            if h == 0:
                square = result_pool.tile([P, TOKENS], F32, name="square_sum")
                square_sum[half] = square
            else:
                square = stage.tile([P, TOKENS], F32, name="square")
            nc.scalar.activation(
                out=square[:],
                in_=acc[:],
                func=ACT.Square,
                bias=bias_col[:, head : head + 1],
                scale=1.0,
            )
            if h > 0:
                nc.gpsimd.tensor_tensor(
                    out=square_sum[half][:], in0=square_sum[half][:], in1=square[:], op=ALU.add
                )

        def rotate(head):
            half, h = divmod(head, HEADS)
            if h == 0:
                rotated[half] = result_pool.tile(
                    [P, TOKEN_TILES, HEADS, HEAD_DIM], F32, name="rotated"
                )
            back = back_pool.tile([P, TOKEN_TILES, HEAD_DIM], F32, name="back")
            for t in range(TOKEN_TILES):
                nc.tensor.transpose(
                    back[:, t, :], scaled_of[head][:, t * P : (t + 1) * P], ident[:]
                )
            straight = stage.tile([P, TOKEN_TILES, HEAD_DIM], F32, name="straight")
            nc.vector.tensor_tensor(out=straight[:], in0=back[:], in1=cos_f[:], op=ALU.mult)
            crossed = stage.tile([P, TOKEN_TILES, HEAD_DIM], F32, name="crossed")
            nc.vector.tensor_tensor(
                out=crossed[:, :, 0:HALF_DIM],
                in0=back[:, :, HALF_DIM:HEAD_DIM],
                in1=sin_signed[:, :, 0:HALF_DIM],
                op=ALU.mult,
            )
            nc.vector.tensor_tensor(
                out=crossed[:, :, HALF_DIM:HEAD_DIM],
                in0=back[:, :, 0:HALF_DIM],
                in1=sin_signed[:, :, HALF_DIM:HEAD_DIM],
                op=ALU.mult,
            )
            nc.vector.tensor_tensor(
                out=rotated[half][:, :, h, :], in0=straight[:], in1=crossed[:], op=ALU.add
            )

        def sum_squares(half):
            sums_back = back_pool.tile([P, TOKEN_TILES, HEAD_DIM], F32, name="back")
            for t in range(TOKEN_TILES):
                nc.tensor.transpose(
                    sums_back[:, t, :], square_sum[half][:, t * P : (t + 1) * P], ident[:]
                )
            total = stage.tile([P, TOKEN_TILES], F32, name="total")
            nc.vector.tensor_reduce(out=total[:], in_=sums_back[:], axis=AXIS.X, op=ALU.add)
            total_of[half] = total

        def inverse_rms(half):
            rms = stage.tile([P, TOKEN_TILES], F32, name="rms")
            nc.scalar.activation(
                out=rms[:],
                in_=total_of[half][:],
                func=ACT.Sqrt,
                bias=eps_col[:, 0:1],
                scale=1.0 / DIM,
            )
            inv_rms = stage.tile([P, TOKEN_TILES], F32, name="inv_rms")
            nc.vector.reciprocal(out=inv_rms[:], in_=rms[:])
            inv_rms_of[half] = inv_rms

        def scale_and_store(half, t):
            row = rotated[half][:, t, :, :].rearrange("p h d -> p (h d)")
            nc.vector.tensor_scalar(
                out=row,
                in0=row,
                scalar1=inv_rms_of[half][:, t : t + 1],
                scalar2=None,
                op0=ALU.mult,
            )
            nc.sync.dma_start(out=outs[half][t * P : (t + 1) * P, :], in_=row)

        LAST_STAGE = 5
        for step in range(ALL_HEADS + LAST_STAGE + TOKEN_TILES):
            if step + PREFETCH < ALL_HEADS:
                load_weights(step + PREFETCH)
            if 0 <= step - 2 < ALL_HEADS:
                quantise(step - 2)
            if 0 <= step - LAST_STAGE < ALL_HEADS:
                rotate(step - LAST_STAGE)
            for half in range(2):
                since = step - LAST_STAGE - (half * HEADS + HEADS - 1)
                if since == 0:
                    sum_squares(half)
                if since == 1:
                    inverse_rms(half)
                if 1 <= since <= TOKEN_TILES:
                    scale_and_store(half, since - 1)
            if 0 <= step - 4 < ALL_HEADS:
                bias_gain_square(step - 4)
            if 0 <= step - 1 < ALL_HEADS:
                regroup_weights(step - 1)
            for pair in range(PASSES // 2):
                if step < ALL_HEADS:
                    flip(step, pair)
                if 0 <= step - 3 < ALL_HEADS:
                    multiply(step - 3, pair)
